import numpy as np
import ml_dtypes


def mxq(x, axis, fmt="e4m3"):
    dtype, down = {"e4m3": (ml_dtypes.float8_e4m3fn, 7), "e5m2": (ml_dtypes.float8_e5m2, 14)}[fmt]
    v = np.moveaxis(np.asarray(x, np.float32).astype(ml_dtypes.bfloat16).astype(np.float64), axis, -1)
    blocks = v.reshape(v.shape[:-1] + (-1, 32))
    amax = np.abs(blocks).max(-1, keepdims=True)
    byte = np.maximum(np.where(amax > 0, np.frexp(amax)[1] - 1 + 127, 0) - down, 1)
    scale = np.exp2(byte - 127.0)
    codes = (blocks / scale).astype(np.float32).astype(dtype).astype(np.float64)
    return np.moveaxis((codes * scale).reshape(v.shape), -1, axis)


WIDE = False


def mx_kscale(k):
    if not WIDE:
        return np.ones(k)
    levels = np.array([10, -10, 5, -5, 0])
    a = np.random.permutation(np.resize(levels, k // 512 * 4)).reshape(k // 512, 4)
    idx = np.arange(k)
    return np.exp2(a[idx // 512, idx % 128 // 32])


BF16 = ml_dtypes.bfloat16


def bf(x):
    return np.asarray(x, np.float32).astype(BF16)


def f64(x):
    return np.asarray(x).astype(np.float64)


B, C, N = 2, 1024, 1024
NH = N // 2
SQRT2 = np.sqrt(2.0)


def haar_approx(x):
    return x.reshape(B, C, NH, 2).sum(-1) / SQRT2


def setup_inputs():
    s = mx_kscale(NH)
    return {"x": bf(np.random.standard_normal((B, C, N)) * np.repeat(s, 2)),
            "Wq": bf(np.random.standard_normal((N, NH)) * 2.0 / np.sqrt(N) / s),
            "bq": bf(np.random.standard_normal(N) * 0.2),
            "Wk": bf(np.random.standard_normal((N, NH)) * 2.0 / np.sqrt(N) / s),
            "bk": bf(np.random.standard_normal(N) * 0.2)}


def reference(x, Wq, bq, Wk, bk):
    hq = mxq(haar_approx(f64(x)), 2, "e4m3")
    q = (hq @ mxq(f64(Wq).T, 0, "e4m3")) + f64(bq)
    k = (hq @ mxq(f64(Wk).T, 0, "e4m3")) + f64(bk)
    return q, k

@@ -1,0 +1,171 @@
+import math
+from contextlib import ExitStack
+
+import concourse.mybir as mybir
+from concourse.masks import make_identity
+
+F32 = mybir.dt.float32
+BF16 = mybir.dt.bfloat16
+U32 = mybir.dt.uint32
+U8 = mybir.dt.uint8
+FP8X4 = mybir.dt.float8_e4m3fn_x4
+ADD = mybir.AluOpType.add
+COPY = mybir.ActivationFunctionType.Copy
+
+P = 128
+PACK = 4
+ROWS = 2048
+SAMPLES = 1024
+COEFFS = SAMPLES // 2
+FEATURES = 1024
+BANK = 512
+ROW_TILES = ROWS // P
+PAIRS = ROW_TILES // 2
+CHUNKS = FEATURES // BANK
+INV_SQRT2 = 1.0 / math.sqrt(2.0)
+
+FLOPS = 2 * ROWS * COEFFS * 2 * FEATURES
+
+
+def tile_wiaa_pa_kernel(tc, x, Wq, bq, Wk, bk, out_q, out_k):
+    nc = tc.nc
+    weights = (Wq, Wk)
+    biases = (bq, bk)
+
+    x_rows = x.flatten_outer_dims().rearrange("(p j) n -> p j n", j=ROW_TILES)
+    out_rows = tuple(
+        o.flatten_outer_dims().rearrange("(p j) f -> p j f", j=ROW_TILES) for o in (out_q, out_k)
+    )
+
+    with ExitStack() as ctx:
+        const = ctx.enter_context(tc.tile_pool(name="const", bufs=1))
+        x_pool = ctx.enter_context(tc.tile_pool(name="x_pool", bufs=PAIRS))
+        w_pool = ctx.enter_context(tc.tile_pool(name="w_pool", bufs=2 * CHUNKS))
+        w_stage = ctx.enter_context(tc.tile_pool(name="w_stage", bufs=2))
+        h_stage = ctx.enter_context(tc.tile_pool(name="h_stage", bufs=4))
+        out_pool = ctx.enter_context(tc.tile_pool(name="out_pool", bufs=4))
+        flip_psum = ctx.enter_context(tc.psum_pool(name="flip_psum", bufs=3))
+        acc_psum = ctx.enter_context(tc.psum_pool(name="acc_psum", bufs=5))
+
+        identity = const.tile([P, P], F32)
+        make_identity(nc, identity[:])
+        ones = const.tile([P, P], BF16)
+        nc.vector.memset(ones[:], 1.0)
+        bias_in = const.tile([1, 2 * FEATURES], BF16)
+        for w in range(2):
+            nc.sync.dma_start(
+                out=bias_in[:, w * FEATURES : (w + 1) * FEATURES],
+                in_=biases[w].rearrange("(o f) -> o f", o=1),
+            )
+        bias_row = const.tile([P, 2 * FEATURES], BF16)
+        nc.vector.memset(bias_row[:], 0.0)
+        nc.vector.tensor_copy(out=bias_row[0:1, :], in_=bias_in[:])
+
+        x_pairs = []
+        w_raws = []
+
+        def load_x(pair):
+            x_pair = x_pool.tile([P, 2, SAMPLES], BF16, name="x_pair")
+            nc.sync.dma_start(out=x_pair[:], in_=x_rows[:, 2 * pair : 2 * pair + 2, :])
+            x_pairs.append(x_pair)
+
+        load_x(0)
+        for w in range(2):
+            w_chunks = weights[w].rearrange("(c a p) i -> c p a i", a=BANK // P, p=P)
+            for c in range(CHUNKS):
+                w_raw = w_pool.tile([P, BANK // P, COEFFS], BF16, name="w_raw")
+                nc.sync.dma_start(out=w_raw[:], in_=w_chunks[c])
+                w_raws.append(w_raw)
+        for pair in range(1, PAIRS):
+            load_x(pair)
+
+        bias_all = const.tile([P, 2 * FEATURES], F32)
+        for b in range(2 * CHUNKS):
+            cols = slice(b * BANK, (b + 1) * BANK)
+            spread = acc_psum.tile([P, BANK], F32, tag="acc")
+            nc.tensor.matmul(out=spread[:], lhsT=ones[:], rhs=bias_row[:, cols], start=True, stop=True)
+            nc.scalar.copy(out=bias_all[:, cols], in_=spread[:])
+
+        def quantise_weight_chunk(w_raw):
+            w_grouped = w_stage.tile([P, BANK * PACK], BF16, align_bytes=64)
+            grouped_words = w_grouped[:].bitcast(F32).rearrange("p (f u) -> p f u", u=2)
+            for half in range(2):
+                flipped = flip_psum.tile([P, 2, 2 * P], F32, tag="flip")
+                for a in range(2):
+                    words = w_raw[:, 2 * half + a, :].bitcast(F32)
+                    for u in range(2):
+                        nc.tensor.transpose(
+                            out=flipped[:, u, a * P : (a + 1) * P],
+                            in_=words[:, u * P : (u + 1) * P],
+                            identity=identity[:],
+                        )
+                dst = grouped_words[:, half * 2 * P : (half + 1) * 2 * P, :]
+                src = flipped[:].rearrange("p u f -> p f u")
+                if half == 0:
+                    nc.vector.tensor_copy(out=dst, in_=src)
+                else:
+                    nc.scalar.copy(out=dst, in_=src)
+            w_codes = w_pool.tile([P, BANK], U32, align_bytes=64, name="w_codes")
+            w_scales = w_pool.tile([P, BANK], U8, align_bytes=64, name="w_scales")
+            nc.vector.quantize_mx(out=w_codes[:].bitcast(FP8X4), scales=w_scales[:], in_=w_grouped[:])
+            return w_codes, w_scales
+
+        def quantise_h(x_pair):
+            h_grouped = h_stage.tile([P, 2 * P * PACK], BF16, align_bytes=64)
+            for j in range(2):
+                samples = x_pair[:, j, :].rearrange("r (u p e s) -> r u e p s", u=2, p=P, e=2, s=2)
+                sums = h_stage.tile([P, COEFFS], F32)
+                nc.gpsimd.tensor_tensor(
+                    out=sums[:].rearrange("r (u e p) -> r u e p", u=2, e=2),
+                    in0=samples[:, :, :, :, 0],
+                    in1=samples[:, :, :, :, 1],
+                    op=ADD,
+                )
+                flipped = flip_psum.tile([P, PACK, P], F32, tag="flip")
+                for t in range(PACK):
+                    nc.tensor.transpose(
+                        out=flipped[:, t, :], in_=sums[:, t * P : (t + 1) * P], identity=identity[:]
+                    )
+                nc.scalar.activation(
+                    out=h_grouped[:, j * P * PACK : (j + 1) * P * PACK].rearrange("p (r t) -> p r t", t=PACK),
+                    in_=flipped[:].rearrange("p t r -> p r t"),
+                    func=COPY,
+                    scale=INV_SQRT2,
+                )
+            h_codes = h_stage.tile([P, 2 * P], U32, align_bytes=64)
+            h_scales = h_stage.tile([P, 2 * P], U8, align_bytes=64)
+            nc.vector.quantize_mx(out=h_codes[:].bitcast(FP8X4), scales=h_scales[:], in_=h_grouped[:])
+            return h_codes, h_scales
+
+        w_quantised = []
+        h_next = quantise_h(x_pairs[0])
+        for pair in range(PAIRS):
+            h_codes, h_scales = h_next
+            if pair + 1 < PAIRS:
+                h_next = quantise_h(x_pairs[pair + 1])
+            for w in range(2):
+                if pair == 0:
+                    for c in range(CHUNKS):
+                        w_quantised.append(quantise_weight_chunk(w_raws[w * CHUNKS + c]))
+                result = out_pool.tile([P, 2, FEATURES], F32)
+                for j in range(2):
+                    rows = slice(j * P, (j + 1) * P)
+                    for c in range(CHUNKS):
+                        w_codes, w_scales = w_quantised[w * CHUNKS + c]
+                        acc = acc_psum.tile([P, BANK], F32, tag="acc")
+                        nc.tensor.matmul_mx(
+                            out=acc[:],
+                            lhsT=h_codes[:, rows].bitcast(FP8X4),
+                            lhsT_scale=h_scales[:, rows],
+                            rhs=w_codes[:].bitcast(FP8X4),
+                            rhs_scale=w_scales[:],
+                            start=True,
+                            stop=True,
+                        )
+                        nc.vector.tensor_tensor(
+                            out=result[:, j, c * BANK : (c + 1) * BANK],
+                            in0=acc[:],
+                            in1=bias_all[:, (w * CHUNKS + c) * BANK : (w * CHUNKS + c + 1) * BANK],
+                            op=ADD,
+                        )
+                nc.sync.dma_start(out=out_rows[w][:, 2 * pair : 2 * pair + 2, :], in_=result[:])

@@ -42,10 +42,13 @@ def tile_wiaa_pa_kernel(tc, x, Wq, bq, Wk, bk, out_q, out_k):
         x_pool = ctx.enter_context(tc.tile_pool(name="x_pool", bufs=PAIRS))
         w_pool = ctx.enter_context(tc.tile_pool(name="w_pool", bufs=2 * CHUNKS))
         w_stage = ctx.enter_context(tc.tile_pool(name="w_stage", bufs=2))
-        h_stage = ctx.enter_context(tc.tile_pool(name="h_stage", bufs=4))
+        sum_pool = ctx.enter_context(tc.tile_pool(name="sum_pool", bufs=6))
+        h_stage = ctx.enter_context(tc.tile_pool(name="h_stage", bufs=3))
         out_pool = ctx.enter_context(tc.tile_pool(name="out_pool", bufs=4))
         flip_psum = ctx.enter_context(tc.psum_pool(name="flip_psum", bufs=3))
         acc_psum = ctx.enter_context(tc.psum_pool(name="acc_psum", bufs=5))
+
+        ctx.enter_context(tc.manual_schedule())
 
         identity = const.tile([P, P], F32)
         make_identity(nc, identity[:])
@@ -69,14 +72,18 @@ def tile_wiaa_pa_kernel(tc, x, Wq, bq, Wk, bk, out_q, out_k):
             nc.sync.dma_start(out=x_pair[:], in_=x_rows[:, 2 * pair : 2 * pair + 2, :])
             x_pairs.append(x_pair)
 
-        load_x(0)
-        for w in range(2):
+        def load_weight(w):
             w_chunks = weights[w].rearrange("(c a p) i -> c p a i", a=BANK // P, p=P)
             for c in range(CHUNKS):
                 w_raw = w_pool.tile([P, BANK // P, COEFFS], BF16, name="w_raw")
                 nc.sync.dma_start(out=w_raw[:], in_=w_chunks[c])
                 w_raws.append(w_raw)
-        for pair in range(1, PAIRS):
+
+        load_x(0)
+        load_weight(0)
+        load_x(1)
+        load_weight(1)
+        for pair in range(2, PAIRS):
             load_x(pair)
 
         bias_all = const.tile([P, 2 * FEATURES], F32)
@@ -84,7 +91,7 @@ def tile_wiaa_pa_kernel(tc, x, Wq, bq, Wk, bk, out_q, out_k):
             cols = slice(b * BANK, (b + 1) * BANK)
             spread = acc_psum.tile([P, BANK], F32, tag="acc")
             nc.tensor.matmul(out=spread[:], lhsT=ones[:], rhs=bias_row[:, cols], start=True, stop=True)
-            nc.scalar.copy(out=bias_all[:, cols], in_=spread[:])
+            nc.vector.tensor_copy(out=bias_all[:, cols], in_=spread[:])
 
         def quantise_weight_chunk(w_raw):
             w_grouped = w_stage.tile([P, BANK * PACK], BF16, align_bytes=64)
@@ -99,32 +106,35 @@ def tile_wiaa_pa_kernel(tc, x, Wq, bq, Wk, bk, out_q, out_k):
                             in_=words[:, u * P : (u + 1) * P],
                             identity=identity[:],
                         )
-                dst = grouped_words[:, half * 2 * P : (half + 1) * 2 * P, :]
-                src = flipped[:].rearrange("p u f -> p f u")
-                if half == 0:
-                    nc.vector.tensor_copy(out=dst, in_=src)
-                else:
-                    nc.scalar.copy(out=dst, in_=src)
+                nc.scalar.copy(
+                    out=grouped_words[:, half * 2 * P : (half + 1) * 2 * P, :],
+                    in_=flipped[:].rearrange("p u f -> p f u"),
+                )
             w_codes = w_pool.tile([P, BANK], U32, align_bytes=64, name="w_codes")
             w_scales = w_pool.tile([P, BANK], U8, align_bytes=64, name="w_scales")
             nc.vector.quantize_mx(out=w_codes[:].bitcast(FP8X4), scales=w_scales[:], in_=w_grouped[:])
             return w_codes, w_scales
 
-        def quantise_h(x_pair):
+        def sum_sample_pairs(pair, j):
+            samples = x_pairs[pair][:, j, :].rearrange("r (u p e s) -> r u e p s", u=2, p=P, e=2, s=2)
+            sums = sum_pool.tile([P, COEFFS], F32, name="sums")
+            nc.gpsimd.tensor_tensor(
+                out=sums[:].rearrange("r (u e p) -> r u e p", u=2, e=2),
+                in0=samples[:, :, :, :, 0],
+                in1=samples[:, :, :, :, 1],
+                op=ADD,
+            )
+            return sums
+
+        def quantise_h(sums_of_pair):
             h_grouped = h_stage.tile([P, 2 * P * PACK], BF16, align_bytes=64)
             for j in range(2):
-                samples = x_pair[:, j, :].rearrange("r (u p e s) -> r u e p s", u=2, p=P, e=2, s=2)
-                sums = h_stage.tile([P, COEFFS], F32)
-                nc.gpsimd.tensor_tensor(
-                    out=sums[:].rearrange("r (u e p) -> r u e p", u=2, e=2),
-                    in0=samples[:, :, :, :, 0],
-                    in1=samples[:, :, :, :, 1],
-                    op=ADD,
-                )
                 flipped = flip_psum.tile([P, PACK, P], F32, tag="flip")
                 for t in range(PACK):
                     nc.tensor.transpose(
-                        out=flipped[:, t, :], in_=sums[:, t * P : (t + 1) * P], identity=identity[:]
+                        out=flipped[:, t, :],
+                        in_=sums_of_pair[j][:, t * P : (t + 1) * P],
+                        identity=identity[:],
                     )
                 nc.scalar.activation(
                     out=h_grouped[:, j * P * PACK : (j + 1) * P * PACK].rearrange("p (r t) -> p r t", t=PACK),
@@ -137,21 +147,25 @@ def tile_wiaa_pa_kernel(tc, x, Wq, bq, Wk, bk, out_q, out_k):
             nc.vector.quantize_mx(out=h_codes[:].bitcast(FP8X4), scales=h_scales[:], in_=h_grouped[:])
             return h_codes, h_scales
 
-        w_quantised = []
-        h_next = quantise_h(x_pairs[0])
+        sums = [[sum_sample_pairs(pair, j) for j in range(2)] for pair in range(2)]
+        w_quantised = [quantise_weight_chunk(w_raws[0])]
+        h_next = quantise_h(sums[0])
+        w_quantised.append(quantise_weight_chunk(w_raws[1]))
+
         for pair in range(PAIRS):
             h_codes, h_scales = h_next
-            if pair + 1 < PAIRS:
-                h_next = quantise_h(x_pairs[pair + 1])
+            sums.append([])
             for w in range(2):
-                if pair == 0:
-                    for c in range(CHUNKS):
-                        w_quantised.append(quantise_weight_chunk(w_raws[w * CHUNKS + c]))
+                if w == 1 and pair + 1 < PAIRS:
+                    h_next = quantise_h(sums[pair + 1])
                 result = out_pool.tile([P, 2, FEATURES], F32)
-                for j in range(2):
-                    rows = slice(j * P, (j + 1) * P)
-                    for c in range(CHUNKS):
-                        w_codes, w_scales = w_quantised[w * CHUNKS + c]
+                for c in range(CHUNKS):
+                    if pair == 0 and w == 0:
+                        w_quantised.append(quantise_weight_chunk(w_raws[CHUNKS + c]))
+                    w_codes, w_scales = w_quantised[w * CHUNKS + c]
+                    bias_cols = bias_all[:, (w * CHUNKS + c) * BANK : (w * CHUNKS + c + 1) * BANK]
+                    for j in range(2):
+                        rows = slice(j * P, (j + 1) * P)
                         acc = acc_psum.tile([P, BANK], F32, tag="acc")
                         nc.tensor.matmul_mx(
                             out=acc[:],
@@ -162,10 +176,12 @@ def tile_wiaa_pa_kernel(tc, x, Wq, bq, Wk, bk, out_q, out_k):
                             start=True,
                             stop=True,
                         )
-                        nc.vector.tensor_tensor(
-                            out=result[:, j, c * BANK : (c + 1) * BANK],
-                            in0=acc[:],
-                            in1=bias_all[:, (w * CHUNKS + c) * BANK : (w * CHUNKS + c + 1) * BANK],
-                            op=ADD,
-                        )
+                        finished = result[:, j, c * BANK : (c + 1) * BANK]
+                        if c == 0 and j == 0:
+                            nc.scalar.copy(out=finished, in_=acc[:])
+                            nc.gpsimd.tensor_tensor(out=finished, in0=finished, in1=bias_cols, op=ADD)
+                        else:
+                            nc.vector.tensor_tensor(out=finished, in0=acc[:], in1=bias_cols, op=ADD)
                 nc.sync.dma_start(out=out_rows[w][:, 2 * pair : 2 * pair + 2, :], in_=result[:])
+                if pair + 2 < PAIRS:
+                    sums[pair + 2].append(sum_sample_pairs(pair + 2, w))

@@ -118,7 +118,8 @@ def tile_wiaa_pa_kernel(tc, x, Wq, bq, Wk, bk, out_q, out_k):
         def sum_sample_pairs(pair, j):
             samples = x_pairs[pair][:, j, :].rearrange("r (u p e s) -> r u e p s", u=2, p=P, e=2, s=2)
             sums = sum_pool.tile([P, COEFFS], F32, name="sums")
-            nc.gpsimd.tensor_tensor(
+            engine = nc.gpsimd if j == 0 else nc.vector
+            engine.tensor_tensor(
                 out=sums[:].rearrange("r (u e p) -> r u e p", u=2, e=2),
                 in0=samples[:, :, :, :, 0],
                 in1=samples[:, :, :, :, 1],
@@ -126,7 +127,7 @@ def tile_wiaa_pa_kernel(tc, x, Wq, bq, Wk, bk, out_q, out_k):
             )
             return sums
 
-        def quantise_h(sums_of_pair):
+        def flip_h(sums_of_pair):
             h_grouped = h_stage.tile([P, 2 * P * PACK], BF16, align_bytes=64)
             for j in range(2):
                 flipped = flip_psum.tile([P, PACK, P], F32, tag="flip")
@@ -142,22 +143,32 @@ def tile_wiaa_pa_kernel(tc, x, Wq, bq, Wk, bk, out_q, out_k):
                     func=COPY,
                     scale=INV_SQRT2,
                 )
+            return h_grouped
+
+        def quantise_h(h_grouped):
             h_codes = h_stage.tile([P, 2 * P], U32, align_bytes=64)
             h_scales = h_stage.tile([P, 2 * P], U8, align_bytes=64)
             nc.vector.quantize_mx(out=h_codes[:].bitcast(FP8X4), scales=h_scales[:], in_=h_grouped[:])
             return h_codes, h_scales
 
-        sums = [[sum_sample_pairs(pair, j) for j in range(2)] for pair in range(2)]
+        sums = [[sum_sample_pairs(0, j) for j in range(2)]]
         w_quantised = [quantise_weight_chunk(w_raws[0])]
-        h_next = quantise_h(sums[0])
+        h_next = quantise_h(flip_h(sums[0]))
         w_quantised.append(quantise_weight_chunk(w_raws[1]))
+        sums.append([sum_sample_pairs(1, j) for j in range(2)])
 
         for pair in range(PAIRS):
             h_codes, h_scales = h_next
             sums.append([])
+            if 0 < pair < PAIRS - 1:
+                h_grouped_next = flip_h(sums[pair + 1])
             for w in range(2):
+                if w == 1 and pair == 0:
+                    h_grouped_next = flip_h(sums[pair + 1])
                 if w == 1 and pair + 1 < PAIRS:
-                    h_next = quantise_h(sums[pair + 1])
+                    h_next = quantise_h(h_grouped_next)
+                if pair + 2 < PAIRS:
+                    sums[pair + 2].append(sum_sample_pairs(pair + 2, w))
                 result = out_pool.tile([P, 2, FEATURES], F32)
                 for c in range(CHUNKS):
                     if pair == 0 and w == 0:
@@ -183,5 +194,3 @@ def tile_wiaa_pa_kernel(tc, x, Wq, bq, Wk, bk, out_q, out_k):
                         else:
                             nc.vector.tensor_tensor(out=finished, in0=acc[:], in1=bias_cols, op=ADD)
                 nc.sync.dma_start(out=out_rows[w][:, 2 * pair : 2 * pair + 2, :], in_=result[:])
-                if pair + 2 < PAIRS:
-                    sums[pair + 2].append(sum_sample_pairs(pair + 2, w))

@@ -52,6 +52,8 @@ def tile_wiaa_pa_kernel(tc, x, Wq, bq, Wk, bk, out_q, out_k):
 
         identity = const.tile([P, P], F32)
         make_identity(nc, identity[:])
+        identity_bf = const.tile([P, P], BF16)
+        nc.vector.tensor_copy(out=identity_bf[:], in_=identity[:])
         ones = const.tile([P, P], BF16)
         nc.vector.memset(ones[:], 1.0)
         bias_in = const.tile([1, 2 * FEATURES], BF16)
@@ -118,8 +120,7 @@ def tile_wiaa_pa_kernel(tc, x, Wq, bq, Wk, bk, out_q, out_k):
         def sum_sample_pairs(pair, j):
             samples = x_pairs[pair][:, j, :].rearrange("r (u p e s) -> r u e p s", u=2, p=P, e=2, s=2)
             sums = sum_pool.tile([P, COEFFS], F32, name="sums")
-            engine = nc.gpsimd if j == 0 else nc.vector
-            engine.tensor_tensor(
+            nc.gpsimd.tensor_tensor(
                 out=sums[:].rearrange("r (u e p) -> r u e p", u=2, e=2),
                 in0=samples[:, :, :, :, 0],
                 in1=samples[:, :, :, :, 1],
@@ -127,16 +128,31 @@ def tile_wiaa_pa_kernel(tc, x, Wq, bq, Wk, bk, out_q, out_k):
             )
             return sums
 
-        def flip_h(sums_of_pair):
+        def summed_by_tensor(pair, j):
+            return j == 1 or pair < 2
+
+        def flip_h(pair):
             h_grouped = h_stage.tile([P, 2 * P * PACK], BF16, align_bytes=64)
             for j in range(2):
                 flipped = flip_psum.tile([P, PACK, P], F32, tag="flip")
-                for t in range(PACK):
-                    nc.tensor.transpose(
-                        out=flipped[:, t, :],
-                        in_=sums_of_pair[j][:, t * P : (t + 1) * P],
-                        identity=identity[:],
-                    )
+                if summed_by_tensor(pair, j):
+                    samples = x_pairs[pair][:, j, :].rearrange("r (u p e s) -> r u e s p", u=2, p=P, e=2, s=2)
+                    for t in range(PACK):
+                        for s in range(2):
+                            nc.tensor.matmul(
+                                out=flipped[:, t, :],
+                                lhsT=samples[:, t // 2, t % 2, s, :],
+                                rhs=identity_bf[:],
+                                start=(s == 0),
+                                stop=(s == 1),
+                            )
+                else:
+                    for t in range(PACK):
+                        nc.tensor.transpose(
+                            out=flipped[:, t, :],
+                            in_=sums[pair][:, t * P : (t + 1) * P],
+                            identity=identity[:],
+                        )
                 nc.scalar.activation(
                     out=h_grouped[:, j * P * PACK : (j + 1) * P * PACK].rearrange("p (r t) -> p r t", t=PACK),
                     in_=flipped[:].rearrange("p t r -> p r t"),
@@ -151,24 +167,22 @@ def tile_wiaa_pa_kernel(tc, x, Wq, bq, Wk, bk, out_q, out_k):
             nc.vector.quantize_mx(out=h_codes[:].bitcast(FP8X4), scales=h_scales[:], in_=h_grouped[:])
             return h_codes, h_scales
 
-        sums = [[sum_sample_pairs(0, j) for j in range(2)]]
+        sums = {}
         w_quantised = [quantise_weight_chunk(w_raws[0])]
-        h_next = quantise_h(flip_h(sums[0]))
+        h_next = quantise_h(flip_h(0))
         w_quantised.append(quantise_weight_chunk(w_raws[1]))
-        sums.append([sum_sample_pairs(1, j) for j in range(2)])
 
         for pair in range(PAIRS):
             h_codes, h_scales = h_next
-            sums.append([])
             if 0 < pair < PAIRS - 1:
-                h_grouped_next = flip_h(sums[pair + 1])
+                h_grouped_next = flip_h(pair + 1)
             for w in range(2):
                 if w == 1 and pair == 0:
-                    h_grouped_next = flip_h(sums[pair + 1])
+                    h_grouped_next = flip_h(pair + 1)
                 if w == 1 and pair + 1 < PAIRS:
                     h_next = quantise_h(h_grouped_next)
-                if pair + 2 < PAIRS:
-                    sums[pair + 2].append(sum_sample_pairs(pair + 2, w))
+                if w == 0 and pair + 2 < PAIRS:
+                    sums[pair + 2] = sum_sample_pairs(pair + 2, 0)
                 result = out_pool.tile([P, 2, FEATURES], F32)
                 for c in range(CHUNKS):
                     if pair == 0 and w == 0:

@@ -39,7 +39,7 @@ def tile_wiaa_pa_kernel(tc, x, Wq, bq, Wk, bk, out_q, out_k):
 
     with ExitStack() as ctx:
         const = ctx.enter_context(tc.tile_pool(name="const", bufs=1))
-        x_pool = ctx.enter_context(tc.tile_pool(name="x_pool", bufs=PAIRS))
+        x_pool = ctx.enter_context(tc.tile_pool(name="x_pool", bufs=1))
         w_pool = ctx.enter_context(tc.tile_pool(name="w_pool", bufs=2 * CHUNKS))
         w_stage = ctx.enter_context(tc.tile_pool(name="w_stage", bufs=2))
         sum_pool = ctx.enter_context(tc.tile_pool(name="sum_pool", bufs=6))
@@ -66,27 +66,27 @@ def tile_wiaa_pa_kernel(tc, x, Wq, bq, Wk, bk, out_q, out_k):
         nc.vector.memset(bias_row[:], 0.0)
         nc.vector.tensor_copy(out=bias_row[0:1, :], in_=bias_in[:])
 
-        x_pairs = []
+        x_tiles = []
         w_raws = []
 
-        def load_x(pair):
-            x_pair = x_pool.tile([P, 2, SAMPLES], BF16, name="x_pair")
-            nc.sync.dma_start(out=x_pair[:], in_=x_rows[:, 2 * pair : 2 * pair + 2, :])
-            x_pairs.append(x_pair)
+        def load_x(first, count):
+            x_group = x_pool.tile([P, count, SAMPLES], BF16, name="x_group%d" % first)
+            nc.sync.dma_start(out=x_group[:], in_=x_rows[:, first : first + count, :])
+            x_tiles.extend(x_group[:, i, :] for i in range(count))
 
         def load_weight(w):
-            w_chunks = weights[w].rearrange("(c a p) i -> c p a i", a=BANK // P, p=P)
+            w_chunks = weights[w].rearrange("(c p a) i -> c p a i", a=BANK // P, p=P)
             for c in range(CHUNKS):
                 w_raw = w_pool.tile([P, BANK // P, COEFFS], BF16, name="w_raw")
                 nc.sync.dma_start(out=w_raw[:], in_=w_chunks[c])
                 w_raws.append(w_raw)
 
-        load_x(0)
+        load_x(0, 2)
         load_weight(0)
-        load_x(1)
+        load_x(2, 2)
         load_weight(1)
-        for pair in range(2, PAIRS):
-            load_x(pair)
+        load_x(4, 4)
+        load_x(8, 8)
 
         bias_all = const.tile([P, 2 * FEATURES], F32)
         for b in range(2 * CHUNKS):
@@ -97,20 +97,20 @@ def tile_wiaa_pa_kernel(tc, x, Wq, bq, Wk, bk, out_q, out_k):
 
         def quantise_weight_chunk(w_raw):
             w_grouped = w_stage.tile([P, BANK * PACK], BF16, align_bytes=64)
-            grouped_words = w_grouped[:].bitcast(F32).rearrange("p (f u) -> p f u", u=2)
+            grouped_words = w_grouped[:].bitcast(F32).rearrange("p (m h v) -> p m h v", h=2, v=4)
             for half in range(2):
-                flipped = flip_psum.tile([P, 2, 2 * P], F32, tag="flip")
+                flipped = flip_psum.tile([P, 4, P], F32, tag="flip")
                 for a in range(2):
                     words = w_raw[:, 2 * half + a, :].bitcast(F32)
                     for u in range(2):
                         nc.tensor.transpose(
-                            out=flipped[:, u, a * P : (a + 1) * P],
+                            out=flipped[:, 2 * a + u, :],
                             in_=words[:, u * P : (u + 1) * P],
                             identity=identity[:],
                         )
                 nc.scalar.copy(
-                    out=grouped_words[:, half * 2 * P : (half + 1) * 2 * P, :],
-                    in_=flipped[:].rearrange("p u f -> p f u"),
+                    out=grouped_words[:, :, half, :],
+                    in_=flipped[:].rearrange("p v m -> p m v"),
                 )
             w_codes = w_pool.tile([P, BANK], U32, align_bytes=64, name="w_codes")
             w_scales = w_pool.tile([P, BANK], U8, align_bytes=64, name="w_scales")
@@ -118,7 +118,7 @@ def tile_wiaa_pa_kernel(tc, x, Wq, bq, Wk, bk, out_q, out_k):
             return w_codes, w_scales
 
         def sum_sample_pairs(pair, j):
-            samples = x_pairs[pair][:, j, :].rearrange("r (u p e s) -> r u e p s", u=2, p=P, e=2, s=2)
+            samples = x_tiles[2 * pair + j].rearrange("r (u p e s) -> r u e p s", u=2, p=P, e=2, s=2)
             sums = sum_pool.tile([P, COEFFS], F32, name="sums")
             nc.gpsimd.tensor_tensor(
                 out=sums[:].rearrange("r (u e p) -> r u e p", u=2, e=2),
@@ -136,7 +136,7 @@ def tile_wiaa_pa_kernel(tc, x, Wq, bq, Wk, bk, out_q, out_k):
             for j in range(2):
                 flipped = flip_psum.tile([P, PACK, P], F32, tag="flip")
                 if summed_by_tensor(pair, j):
-                    samples = x_pairs[pair][:, j, :].rearrange("r (u p e s) -> r u e s p", u=2, p=P, e=2, s=2)
+                    samples = x_tiles[2 * pair + j].rearrange("r (u p e s) -> r u e s p", u=2, p=P, e=2, s=2)
                     for t in range(PACK):
                         for s in range(2):
                             nc.tensor.matmul(

@@ -24,6 +24,9 @@ PAIRS = ROW_TILES // 2
 CHUNKS = FEATURES // BANK
 INV_SQRT2 = 1.0 / math.sqrt(2.0)
 
+SUMMED_BY_VECTOR = (0,)
+SUMMED_BY_GPSIMD = (1, 2, 3, 14, 15)
+
 FLOPS = 2 * ROWS * COEFFS * 2 * FEATURES
 
 
@@ -42,30 +45,20 @@ def tile_wiaa_pa_kernel(tc, x, Wq, bq, Wk, bk, out_q, out_k):
         x_pool = ctx.enter_context(tc.tile_pool(name="x_pool", bufs=1))
         w_pool = ctx.enter_context(tc.tile_pool(name="w_pool", bufs=2 * CHUNKS))
         w_stage = ctx.enter_context(tc.tile_pool(name="w_stage", bufs=2))
-        sum_pool = ctx.enter_context(tc.tile_pool(name="sum_pool", bufs=6))
-        h_stage = ctx.enter_context(tc.tile_pool(name="h_stage", bufs=3))
-        out_pool = ctx.enter_context(tc.tile_pool(name="out_pool", bufs=4))
-        flip_psum = ctx.enter_context(tc.psum_pool(name="flip_psum", bufs=3))
-        acc_psum = ctx.enter_context(tc.psum_pool(name="acc_psum", bufs=5))
+        sum_pool = ctx.enter_context(tc.tile_pool(name="sum_pool", bufs=4))
+        h_stage = ctx.enter_context(tc.tile_pool(name="h_stage", bufs=4))
+        out_pool = ctx.enter_context(tc.tile_pool(name="out_pool", bufs=10))
+        flip_psum = ctx.enter_context(tc.psum_pool(name="flip_psum", bufs=4))
+        acc_psum = ctx.enter_context(tc.psum_pool(name="acc_psum", bufs=4))
 
         ctx.enter_context(tc.manual_schedule())
 
-        identity = const.tile([P, P], F32)
-        make_identity(nc, identity[:])
-        identity_bf = const.tile([P, P], BF16)
-        nc.vector.tensor_copy(out=identity_bf[:], in_=identity[:])
-        ones = const.tile([P, P], BF16)
-        nc.vector.memset(ones[:], 1.0)
         bias_in = const.tile([1, 2 * FEATURES], BF16)
         for w in range(2):
             nc.sync.dma_start(
                 out=bias_in[:, w * FEATURES : (w + 1) * FEATURES],
                 in_=biases[w].rearrange("(o f) -> o f", o=1),
             )
-        bias_row = const.tile([P, 2 * FEATURES], BF16)
-        nc.vector.memset(bias_row[:], 0.0)
-        nc.vector.tensor_copy(out=bias_row[0:1, :], in_=bias_in[:])
-
         x_tiles = []
         w_raws = []
 
@@ -74,137 +67,203 @@ def tile_wiaa_pa_kernel(tc, x, Wq, bq, Wk, bk, out_q, out_k):
             nc.sync.dma_start(out=x_group[:], in_=x_rows[:, first : first + count, :])
             x_tiles.extend(x_group[:, i, :] for i in range(count))
 
-        def load_weight(w):
+        def load_weight(w, c):
             w_chunks = weights[w].rearrange("(c p a) i -> c p a i", a=BANK // P, p=P)
-            for c in range(CHUNKS):
-                w_raw = w_pool.tile([P, BANK // P, COEFFS], BF16, name="w_raw")
-                nc.sync.dma_start(out=w_raw[:], in_=w_chunks[c])
-                w_raws.append(w_raw)
+            w_raw = w_pool.tile([P, BANK // P, COEFFS], BF16, name="w_raw")
+            nc.sync.dma_start(out=w_raw[:], in_=w_chunks[c])
+            w_raws.append(w_raw)
 
+        load_weight(0, 0)
         load_x(0, 2)
-        load_weight(0)
+        load_weight(0, 1)
         load_x(2, 2)
-        load_weight(1)
+        load_weight(1, 0)
+        load_weight(1, 1)
         load_x(4, 4)
         load_x(8, 8)
 
+        identity_bf = const.tile([P, P], BF16)
+        make_identity(nc, identity_bf[:])
+        identity = const.tile([P, P], F32)
+        ones = const.tile([P, P], BF16)
+        nc.vector.memset(ones[:], 1.0)
+        bias_row = const.tile([P, 2 * FEATURES], BF16)
+        nc.vector.memset(bias_row[:].bitcast(F32), 0.0)
+        nc.vector.tensor_copy(out=identity[:], in_=identity_bf[:])
+        nc.vector.tensor_copy(out=bias_row[0:1, :], in_=bias_in[:])
         bias_all = const.tile([P, 2 * FEATURES], F32)
-        for b in range(2 * CHUNKS):
+
+        def copy_out(engine, out, in_):
+            if engine is nc.scalar:
+                nc.scalar.copy(out=out, in_=in_)
+            else:
+                nc.vector.tensor_copy(out=out, in_=in_)
+
+        def spread_bias(b, engine):
             cols = slice(b * BANK, (b + 1) * BANK)
             spread = acc_psum.tile([P, BANK], F32, tag="acc")
             nc.tensor.matmul(out=spread[:], lhsT=ones[:], rhs=bias_row[:, cols], start=True, stop=True)
-            nc.vector.tensor_copy(out=bias_all[:, cols], in_=spread[:])
+            copy_out(engine, bias_all[:, cols], spread[:])
 
-        def quantise_weight_chunk(w_raw):
-            w_grouped = w_stage.tile([P, BANK * PACK], BF16, align_bytes=64)
-            grouped_words = w_grouped[:].bitcast(F32).rearrange("p (m h v) -> p m h v", h=2, v=4)
-            for half in range(2):
-                flipped = flip_psum.tile([P, 4, P], F32, tag="flip")
-                for a in range(2):
-                    words = w_raw[:, 2 * half + a, :].bitcast(F32)
-                    for u in range(2):
-                        nc.tensor.transpose(
-                            out=flipped[:, 2 * a + u, :],
-                            in_=words[:, u * P : (u + 1) * P],
-                            identity=identity[:],
-                        )
-                nc.scalar.copy(
-                    out=grouped_words[:, :, half, :],
-                    in_=flipped[:].rearrange("p v m -> p m v"),
-                )
+        w_grouped_tiles = {}
+        w_quantised = {}
+
+        def flip_weight(chunk, half, engine):
+            if half == 0:
+                w_grouped_tiles[chunk] = w_stage.tile([P, BANK * PACK], BF16, align_bytes=64, name="w_grouped")
+            grouped_words = w_grouped_tiles[chunk][:].bitcast(F32).rearrange("p (m h v) -> p m h v", h=2, v=4)
+            flipped = flip_psum.tile([P, 4, P], F32, tag="flip")
+            for a in range(2):
+                words = w_raws[chunk][:, 2 * half + a, :].bitcast(F32)
+                for u in range(2):
+                    nc.tensor.transpose(
+                        out=flipped[:, 2 * a + u, :],
+                        in_=words[:, u * P : (u + 1) * P],
+                        identity=identity[:],
+                    )
+            copy_out(engine, grouped_words[:, :, half, :], flipped[:].rearrange("p v m -> p m v"))
+
+        def quantise_weight(chunk):
             w_codes = w_pool.tile([P, BANK], U32, align_bytes=64, name="w_codes")
             w_scales = w_pool.tile([P, BANK], U8, align_bytes=64, name="w_scales")
-            nc.vector.quantize_mx(out=w_codes[:].bitcast(FP8X4), scales=w_scales[:], in_=w_grouped[:])
-            return w_codes, w_scales
+            nc.vector.quantize_mx(
+                out=w_codes[:].bitcast(FP8X4), scales=w_scales[:], in_=w_grouped_tiles[chunk][:]
+            )
+            w_quantised[chunk] = (w_codes, w_scales)
 
-        def sum_sample_pairs(pair, j):
-            samples = x_tiles[2 * pair + j].rearrange("r (u p e s) -> r u e p s", u=2, p=P, e=2, s=2)
-            sums = sum_pool.tile([P, COEFFS], F32, name="sums")
-            nc.gpsimd.tensor_tensor(
-                out=sums[:].rearrange("r (u e p) -> r u e p", u=2, e=2),
+        sums = {}
+
+        def sum_sample_pairs(tile):
+            samples = x_tiles[tile].rearrange("r (u p e s) -> r u e p s", u=2, p=P, e=2, s=2)
+            sums[tile] = sum_pool.tile([P, COEFFS], F32, name="sums")
+            engine = nc.vector if tile in SUMMED_BY_VECTOR else nc.gpsimd
+            engine.tensor_tensor(
+                out=sums[tile][:].rearrange("r (u e p) -> r u e p", u=2, e=2),
                 in0=samples[:, :, :, :, 0],
                 in1=samples[:, :, :, :, 1],
                 op=ADD,
             )
-            return sums
 
-        def summed_by_tensor(pair, j):
-            return j == 1 or pair < 2
+        h_grouped_tiles = {}
+        h_quantised = {}
 
-        def flip_h(pair):
-            h_grouped = h_stage.tile([P, 2 * P * PACK], BF16, align_bytes=64)
-            for j in range(2):
-                flipped = flip_psum.tile([P, PACK, P], F32, tag="flip")
-                if summed_by_tensor(pair, j):
-                    samples = x_tiles[2 * pair + j].rearrange("r (u p e s) -> r u e s p", u=2, p=P, e=2, s=2)
-                    for t in range(PACK):
-                        for s in range(2):
-                            nc.tensor.matmul(
-                                out=flipped[:, t, :],
-                                lhsT=samples[:, t // 2, t % 2, s, :],
-                                rhs=identity_bf[:],
-                                start=(s == 0),
-                                stop=(s == 1),
-                            )
-                else:
-                    for t in range(PACK):
-                        nc.tensor.transpose(
+        def flip_h(tile):
+            pair, j = divmod(tile, 2)
+            if j == 0:
+                h_grouped_tiles[pair] = h_stage.tile([P, 2 * P * PACK], BF16, align_bytes=64, name="h_grouped")
+            h_grouped = h_grouped_tiles[pair]
+            flipped = flip_psum.tile([P, PACK, P], F32, tag="flip")
+            if tile in sums:
+                for t in range(PACK):
+                    nc.tensor.transpose(
+                        out=flipped[:, t, :],
+                        in_=sums[tile][:, t * P : (t + 1) * P],
+                        identity=identity[:],
+                    )
+            else:
+                samples = x_tiles[tile].rearrange("r (u p e s) -> r u e s p", u=2, p=P, e=2, s=2)
+                for t in range(PACK):
+                    for s in range(2):
+                        nc.tensor.matmul(
                             out=flipped[:, t, :],
-                            in_=sums[pair][:, t * P : (t + 1) * P],
-                            identity=identity[:],
+                            lhsT=samples[:, t // 2, t % 2, s, :],
+                            rhs=identity_bf[:],
+                            start=(s == 0),
+                            stop=(s == 1),
                         )
-                nc.scalar.activation(
-                    out=h_grouped[:, j * P * PACK : (j + 1) * P * PACK].rearrange("p (r t) -> p r t", t=PACK),
-                    in_=flipped[:].rearrange("p t r -> p r t"),
-                    func=COPY,
-                    scale=INV_SQRT2,
-                )
-            return h_grouped
+            nc.scalar.activation(
+                out=h_grouped[:, j * P * PACK : (j + 1) * P * PACK].rearrange("p (r t) -> p r t", t=PACK),
+                in_=flipped[:].rearrange("p t r -> p r t"),
+                func=COPY,
+                scale=INV_SQRT2,
+            )
 
-        def quantise_h(h_grouped):
-            h_codes = h_stage.tile([P, 2 * P], U32, align_bytes=64)
-            h_scales = h_stage.tile([P, 2 * P], U8, align_bytes=64)
-            nc.vector.quantize_mx(out=h_codes[:].bitcast(FP8X4), scales=h_scales[:], in_=h_grouped[:])
-            return h_codes, h_scales
+        def quantise_h(pair):
+            h_codes = h_stage.tile([P, 2 * P], U32, align_bytes=64, name="h_codes")
+            h_scales = h_stage.tile([P, 2 * P], U8, align_bytes=64, name="h_scales")
+            nc.vector.quantize_mx(
+                out=h_codes[:].bitcast(FP8X4), scales=h_scales[:], in_=h_grouped_tiles[pair][:]
+            )
+            h_quantised[pair] = (h_codes, h_scales)
 
-        sums = {}
-        w_quantised = [quantise_weight_chunk(w_raws[0])]
-        h_next = quantise_h(flip_h(0))
-        w_quantised.append(quantise_weight_chunk(w_raws[1]))
+        results = {}
 
-        for pair in range(PAIRS):
-            h_codes, h_scales = h_next
-            if 0 < pair < PAIRS - 1:
-                h_grouped_next = flip_h(pair + 1)
-            for w in range(2):
-                if w == 1 and pair == 0:
-                    h_grouped_next = flip_h(pair + 1)
-                if w == 1 and pair + 1 < PAIRS:
-                    h_next = quantise_h(h_grouped_next)
-                if w == 0 and pair + 2 < PAIRS:
-                    sums[pair + 2] = sum_sample_pairs(pair + 2, 0)
-                result = out_pool.tile([P, 2, FEATURES], F32)
-                for c in range(CHUNKS):
-                    if pair == 0 and w == 0:
-                        w_quantised.append(quantise_weight_chunk(w_raws[CHUNKS + c]))
-                    w_codes, w_scales = w_quantised[w * CHUNKS + c]
-                    bias_cols = bias_all[:, (w * CHUNKS + c) * BANK : (w * CHUNKS + c + 1) * BANK]
-                    for j in range(2):
-                        rows = slice(j * P, (j + 1) * P)
-                        acc = acc_psum.tile([P, BANK], F32, tag="acc")
-                        nc.tensor.matmul_mx(
-                            out=acc[:],
-                            lhsT=h_codes[:, rows].bitcast(FP8X4),
-                            lhsT_scale=h_scales[:, rows],
-                            rhs=w_codes[:].bitcast(FP8X4),
-                            rhs_scale=w_scales[:],
-                            start=True,
-                            stop=True,
-                        )
-                        finished = result[:, j, c * BANK : (c + 1) * BANK]
-                        if c == 0 and j == 0:
-                            nc.scalar.copy(out=finished, in_=acc[:])
-                            nc.gpsimd.tensor_tensor(out=finished, in0=finished, in1=bias_cols, op=ADD)
-                        else:
-                            nc.vector.tensor_tensor(out=finished, in0=acc[:], in1=bias_cols, op=ADD)
-                nc.sync.dma_start(out=out_rows[w][:, 2 * pair : 2 * pair + 2, :], in_=result[:])
+        def product(pair, w, c, j, engine):
+            h_codes, h_scales = h_quantised[pair]
+            w_codes, w_scales = w_quantised[w * CHUNKS + c]
+            bias_cols = bias_all[:, (w * CHUNKS + c) * BANK : (w * CHUNKS + c + 1) * BANK]
+            rows = slice(j * P, (j + 1) * P)
+            if (pair, w) not in results:
+                results[pair, w] = out_pool.tile([P, 2, FEATURES], F32, name="result")
+            acc = acc_psum.tile([P, BANK], F32, tag="acc")
+            nc.tensor.matmul_mx(
+                out=acc[:],
+                lhsT=h_codes[:, rows].bitcast(FP8X4),
+                lhsT_scale=h_scales[:, rows],
+                rhs=w_codes[:].bitcast(FP8X4),
+                rhs_scale=w_scales[:],
+                start=True,
+                stop=True,
+            )
+            finished = results[pair, w][:, j, c * BANK : (c + 1) * BANK]
+            if engine is nc.scalar:
+                nc.scalar.copy(out=finished, in_=acc[:])
+                nc.gpsimd.tensor_tensor(out=finished, in0=finished, in1=bias_cols, op=ADD)
+            else:
+                nc.vector.tensor_tensor(out=finished, in0=acc[:], in1=bias_cols, op=ADD)
+
+        def store(pair, w):
+            nc.sync.dma_start(out=out_rows[w][:, 2 * pair : 2 * pair + 2, :], in_=results[pair, w][:])
+
+        spread_bias(0, nc.scalar)
+        spread_bias(1, nc.scalar)
+        for tile in range(4):
+            sum_sample_pairs(tile)
+        flip_weight(0, 0, nc.vector)
+        flip_weight(0, 1, nc.scalar)
+        flip_h(0)
+        quantise_weight(0)
+        flip_h(1)
+        quantise_h(0)
+        flip_weight(1, 0, nc.vector)
+        flip_weight(1, 1, nc.scalar)
+        product(0, 0, 0, 0, nc.scalar)
+        quantise_weight(1)
+        product(0, 0, 0, 1, nc.vector)
+        flip_h(2)
+        flip_h(3)
+        product(0, 0, 1, 0, nc.vector)
+        product(0, 0, 1, 1, nc.vector)
+        store(0, 0)
+        flip_weight(2, 0, nc.scalar)
+        quantise_h(1)
+        flip_weight(2, 1, nc.scalar)
+        product(1, 0, 0, 0, nc.vector)
+        product(1, 0, 0, 1, nc.scalar)
+        quantise_weight(2)
+        flip_weight(3, 0, nc.vector)
+        product(1, 0, 1, 0, nc.vector)
+        product(1, 0, 1, 1, nc.vector)
+        store(1, 0)
+        flip_weight(3, 1, nc.scalar)
+        spread_bias(2, nc.scalar)
+        spread_bias(3, nc.scalar)
+        quantise_weight(3)
+
+        steps = [(2 * g + i, w) for g in range(PAIRS // 2) for w in range(2) for i in range(2)]
+        made_at = {steps.index((pair, 0)) - 1: pair for pair in range(2, PAIRS)}
+        for step in range(2, len(steps)):
+            pair, w = steps[step]
+            later = made_at.get(step + 2, 0)
+            for tile in (2 * later, 2 * later + 1):
+                if later and tile in SUMMED_BY_GPSIMD:
+                    sum_sample_pairs(tile)
+            if step in made_at:
+                flip_h(2 * made_at[step])
+                flip_h(2 * made_at[step] + 1)
+            for c in range(CHUNKS):
+                for j in range(2):
+                    product(pair, w, c, j, nc.vector if c or j else nc.scalar)
+                if c == 0 and step in made_at:
+                    quantise_h(made_at[step])
+            store(pair, w)

@@ -24,8 +24,7 @@ PAIRS = ROW_TILES // 2
 CHUNKS = FEATURES // BANK
 INV_SQRT2 = 1.0 / math.sqrt(2.0)
 
-SUMMED_BY_VECTOR = (0,)
-SUMMED_BY_GPSIMD = (1, 2, 3, 14, 15)
+SUMMED_BY_GPSIMD = (8, 10, 12, 14)
 
 FLOPS = 2 * ROWS * COEFFS * 2 * FEATURES
 
@@ -53,11 +52,11 @@ def tile_wiaa_pa_kernel(tc, x, Wq, bq, Wk, bk, out_q, out_k):
 
         ctx.enter_context(tc.manual_schedule())
 
-        bias_in = const.tile([1, 2 * FEATURES], BF16)
+        bias_in = const.tile([2 * FEATURES // P, P], BF16)
         for w in range(2):
             nc.sync.dma_start(
-                out=bias_in[:, w * FEATURES : (w + 1) * FEATURES],
-                in_=biases[w].rearrange("(o f) -> o f", o=1),
+                out=bias_in[w * FEATURES // P : (w + 1) * FEATURES // P, :],
+                in_=biases[w].rearrange("(r f) -> r f", f=P),
             )
         x_tiles = []
         w_raws = []
@@ -73,8 +72,8 @@ def tile_wiaa_pa_kernel(tc, x, Wq, bq, Wk, bk, out_q, out_k):
             nc.sync.dma_start(out=w_raw[:], in_=w_chunks[c])
             w_raws.append(w_raw)
 
-        load_weight(0, 0)
         load_x(0, 2)
+        load_weight(0, 0)
         load_weight(0, 1)
         load_x(2, 2)
         load_weight(1, 0)
@@ -85,13 +84,12 @@ def tile_wiaa_pa_kernel(tc, x, Wq, bq, Wk, bk, out_q, out_k):
         identity_bf = const.tile([P, P], BF16)
         make_identity(nc, identity_bf[:])
         identity = const.tile([P, P], F32)
-        ones = const.tile([P, P], BF16)
-        nc.vector.memset(ones[:], 1.0)
-        bias_row = const.tile([P, 2 * FEATURES], BF16)
-        nc.vector.memset(bias_row[:].bitcast(F32), 0.0)
+        bias_rows = const.tile([P, P], BF16)
+        nc.vector.memset(bias_rows[:], 0.0)
         nc.vector.tensor_copy(out=identity[:], in_=identity_bf[:])
-        nc.vector.tensor_copy(out=bias_row[0:1, :], in_=bias_in[:])
-        bias_all = const.tile([P, 2 * FEATURES], F32)
+        nc.vector.tensor_copy(out=bias_rows[0 : 2 * FEATURES // P, :], in_=bias_in[:])
+        bias_columns = const.tile([P, P], BF16)
+        bias_all = const.tile([P, 2 * FEATURES], BF16)
 
         def copy_out(engine, out, in_):
             if engine is nc.scalar:
@@ -99,11 +97,21 @@ def tile_wiaa_pa_kernel(tc, x, Wq, bq, Wk, bk, out_q, out_k):
             else:
                 nc.vector.tensor_copy(out=out, in_=in_)
 
-        def spread_bias(b, engine):
-            cols = slice(b * BANK, (b + 1) * BANK)
-            spread = acc_psum.tile([P, BANK], F32, tag="acc")
-            nc.tensor.matmul(out=spread[:], lhsT=ones[:], rhs=bias_row[:, cols], start=True, stop=True)
-            copy_out(engine, bias_all[:, cols], spread[:])
+        def turn_bias():
+            turned = acc_psum.tile([P, P], BF16, tag="acc")
+            nc.tensor.transpose(out=turned[:], in_=bias_rows[:], identity=identity_bf[:])
+            nc.vector.tensor_copy(out=bias_columns[:], in_=turned[:])
+
+        def spread_bias(w):
+            spread = acc_psum.tile([P, FEATURES], BF16, tag="acc")
+            for r in range(FEATURES // P):
+                column = w * FEATURES // P + r
+                nc.tensor.transpose(
+                    out=spread[:, r * P : (r + 1) * P],
+                    in_=bias_columns[:, column : column + 1].to_broadcast([P, P]),
+                    identity=identity_bf[:],
+                )
+            nc.vector.tensor_copy(out=bias_all[:, w * FEATURES : (w + 1) * FEATURES], in_=spread[:])
 
         w_grouped_tiles = {}
         w_quantised = {}
@@ -136,8 +144,7 @@ def tile_wiaa_pa_kernel(tc, x, Wq, bq, Wk, bk, out_q, out_k):
         def sum_sample_pairs(tile):
             samples = x_tiles[tile].rearrange("r (u p e s) -> r u e p s", u=2, p=P, e=2, s=2)
             sums[tile] = sum_pool.tile([P, COEFFS], F32, name="sums")
-            engine = nc.vector if tile in SUMMED_BY_VECTOR else nc.gpsimd
-            engine.tensor_tensor(
+            nc.gpsimd.tensor_tensor(
                 out=sums[tile][:].rearrange("r (u e p) -> r u e p", u=2, e=2),
                 in0=samples[:, :, :, :, 0],
                 in1=samples[:, :, :, :, 1],
@@ -215,18 +222,16 @@ def tile_wiaa_pa_kernel(tc, x, Wq, bq, Wk, bk, out_q, out_k):
         def store(pair, w):
             nc.sync.dma_start(out=out_rows[w][:, 2 * pair : 2 * pair + 2, :], in_=results[pair, w][:])
 
-        spread_bias(0, nc.scalar)
-        spread_bias(1, nc.scalar)
-        for tile in range(4):
-            sum_sample_pairs(tile)
-        flip_weight(0, 0, nc.vector)
-        flip_weight(0, 1, nc.scalar)
+        turn_bias()
         flip_h(0)
-        quantise_weight(0)
+        flip_weight(0, 0, nc.vector)
         flip_h(1)
+        flip_weight(0, 1, nc.scalar)
         quantise_h(0)
-        flip_weight(1, 0, nc.vector)
+        quantise_weight(0)
+        flip_weight(1, 0, nc.scalar)
         flip_weight(1, 1, nc.scalar)
+        spread_bias(0)
         product(0, 0, 0, 0, nc.scalar)
         quantise_weight(1)
         product(0, 0, 0, 1, nc.vector)
@@ -239,31 +244,40 @@ def tile_wiaa_pa_kernel(tc, x, Wq, bq, Wk, bk, out_q, out_k):
         quantise_h(1)
         flip_weight(2, 1, nc.scalar)
         product(1, 0, 0, 0, nc.vector)
-        product(1, 0, 0, 1, nc.scalar)
+        flip_weight(3, 0, nc.scalar)
+        flip_weight(3, 1, nc.scalar)
         quantise_weight(2)
-        flip_weight(3, 0, nc.vector)
+        product(1, 0, 0, 1, nc.vector)
         product(1, 0, 1, 0, nc.vector)
+        quantise_weight(3)
         product(1, 0, 1, 1, nc.vector)
         store(1, 0)
-        flip_weight(3, 1, nc.scalar)
-        spread_bias(2, nc.scalar)
-        spread_bias(3, nc.scalar)
-        quantise_weight(3)
+        spread_bias(1)
+        product(0, 1, 0, 0, nc.scalar)
+        product(0, 1, 0, 1, nc.vector)
+        flip_h(4)
+        flip_h(5)
+        product(0, 1, 1, 0, nc.vector)
+        product(0, 1, 1, 1, nc.vector)
+        store(0, 1)
+        quantise_h(2)
+        product(1, 1, 0, 0, nc.scalar)
+        product(1, 1, 0, 1, nc.vector)
+        product(1, 1, 1, 0, nc.vector)
+        product(1, 1, 1, 1, nc.vector)
+        store(1, 1)
 
-        steps = [(2 * g + i, w) for g in range(PAIRS // 2) for w in range(2) for i in range(2)]
-        made_at = {steps.index((pair, 0)) - 1: pair for pair in range(2, PAIRS)}
-        for step in range(2, len(steps)):
-            pair, w = steps[step]
-            later = made_at.get(step + 2, 0)
-            for tile in (2 * later, 2 * later + 1):
-                if later and tile in SUMMED_BY_GPSIMD:
-                    sum_sample_pairs(tile)
-            if step in made_at:
-                flip_h(2 * made_at[step])
-                flip_h(2 * made_at[step] + 1)
-            for c in range(CHUNKS):
-                for j in range(2):
-                    product(pair, w, c, j, nc.vector if c or j else nc.scalar)
-                if c == 0 and step in made_at:
-                    quantise_h(made_at[step])
-            store(pair, w)
+        for pair in range(2, PAIRS):
+            for w in range(2):
+                if w == 0 and pair + 1 < PAIRS:
+                    flip_h(2 * pair + 2)
+                    flip_h(2 * pair + 3)
+                if w == 1 and pair + 1 < PAIRS:
+                    quantise_h(pair + 1)
+                if w == 0 and 2 * pair + 4 in SUMMED_BY_GPSIMD:
+                    sum_sample_pairs(2 * pair + 4)
+                for c in range(CHUNKS):
+                    for j in range(2):
+                        on_scalar = j == 0 and (c == 0 or (w == 1 and pair % 2 == 1 and pair + 1 < PAIRS))
+                        product(pair, w, c, j, nc.scalar if on_scalar else nc.vector)
+                store(pair, w)

@@ -52,12 +52,6 @@ def tile_wiaa_pa_kernel(tc, x, Wq, bq, Wk, bk, out_q, out_k):
 
         ctx.enter_context(tc.manual_schedule())
 
-        bias_in = const.tile([2 * FEATURES // P, P], BF16)
-        for w in range(2):
-            nc.sync.dma_start(
-                out=bias_in[w * FEATURES // P : (w + 1) * FEATURES // P, :],
-                in_=biases[w].rearrange("(r f) -> r f", f=P),
-            )
         x_tiles = []
         w_raws = []
 
@@ -72,8 +66,15 @@ def tile_wiaa_pa_kernel(tc, x, Wq, bq, Wk, bk, out_q, out_k):
             nc.sync.dma_start(out=w_raw[:], in_=w_chunks[c])
             w_raws.append(w_raw)
 
-        load_x(0, 2)
+        load_x(0, 1)
+        bias_in = const.tile([2 * FEATURES // P, P], BF16)
+        for w in range(2):
+            nc.sync.dma_start(
+                out=bias_in[w * FEATURES // P : (w + 1) * FEATURES // P, :],
+                in_=biases[w].rearrange("(r f) -> r f", f=P),
+            )
         load_weight(0, 0)
+        load_x(1, 1)
         load_weight(0, 1)
         load_x(2, 2)
         load_weight(1, 0)
@@ -87,7 +88,6 @@ def tile_wiaa_pa_kernel(tc, x, Wq, bq, Wk, bk, out_q, out_k):
         bias_rows = const.tile([P, P], BF16)
         nc.vector.memset(bias_rows[:], 0.0)
         nc.vector.tensor_copy(out=identity[:], in_=identity_bf[:])
-        nc.vector.tensor_copy(out=bias_rows[0 : 2 * FEATURES // P, :], in_=bias_in[:])
         bias_columns = const.tile([P, P], BF16)
         bias_all = const.tile([P, 2 * FEATURES], BF16)
 
@@ -98,6 +98,7 @@ def tile_wiaa_pa_kernel(tc, x, Wq, bq, Wk, bk, out_q, out_k):
                 nc.vector.tensor_copy(out=out, in_=in_)
 
         def turn_bias():
+            nc.vector.tensor_copy(out=bias_rows[0 : 2 * FEATURES // P, :], in_=bias_in[:])
             turned = acc_psum.tile([P, P], BF16, tag="acc")
             nc.tensor.transpose(out=turned[:], in_=bias_rows[:], identity=identity_bf[:])
             nc.vector.tensor_copy(out=bias_columns[:], in_=turned[:])
@@ -111,7 +112,7 @@ def tile_wiaa_pa_kernel(tc, x, Wq, bq, Wk, bk, out_q, out_k):
                     in_=bias_columns[:, column : column + 1].to_broadcast([P, P]),
                     identity=identity_bf[:],
                 )
-            nc.vector.tensor_copy(out=bias_all[:, w * FEATURES : (w + 1) * FEATURES], in_=spread[:])
+            nc.scalar.copy(out=bias_all[:, w * FEATURES : (w + 1) * FEATURES], in_=spread[:])
 
         w_grouped_tiles = {}
         w_quantised = {}
@@ -151,14 +152,19 @@ def tile_wiaa_pa_kernel(tc, x, Wq, bq, Wk, bk, out_q, out_k):
                 op=ADD,
             )
 
+        def h_group(tile):
+            return (tile,) if tile < 2 else (tile - tile % 2, tile - tile % 2 + 1)
+
         h_grouped_tiles = {}
         h_quantised = {}
 
         def flip_h(tile):
-            pair, j = divmod(tile, 2)
-            if j == 0:
-                h_grouped_tiles[pair] = h_stage.tile([P, 2 * P * PACK], BF16, align_bytes=64, name="h_grouped")
-            h_grouped = h_grouped_tiles[pair]
+            group = h_group(tile)
+            if tile == group[0]:
+                name = "h_grouped%d" % len(group)
+                h_grouped_tiles[group] = h_stage.tile([P, len(group) * P * PACK], BF16, align_bytes=64, name=name)
+            h_grouped = h_grouped_tiles[group]
+            i = tile - group[0]
             flipped = flip_psum.tile([P, PACK, P], F32, tag="flip")
             if tile in sums:
                 for t in range(PACK):
@@ -179,34 +185,35 @@ def tile_wiaa_pa_kernel(tc, x, Wq, bq, Wk, bk, out_q, out_k):
                             stop=(s == 1),
                         )
             nc.scalar.activation(
-                out=h_grouped[:, j * P * PACK : (j + 1) * P * PACK].rearrange("p (r t) -> p r t", t=PACK),
+                out=h_grouped[:, i * P * PACK : (i + 1) * P * PACK].rearrange("p (r t) -> p r t", t=PACK),
                 in_=flipped[:].rearrange("p t r -> p r t"),
                 func=COPY,
                 scale=INV_SQRT2,
             )
 
-        def quantise_h(pair):
-            h_codes = h_stage.tile([P, 2 * P], U32, align_bytes=64, name="h_codes")
-            h_scales = h_stage.tile([P, 2 * P], U8, align_bytes=64, name="h_scales")
+        def quantise_h(tile):
+            group = h_group(tile)
+            h_codes = h_stage.tile([P, len(group) * P], U32, align_bytes=64, name="h_codes%d" % len(group))
+            h_scales = h_stage.tile([P, len(group) * P], U8, align_bytes=64, name="h_scales%d" % len(group))
             nc.vector.quantize_mx(
-                out=h_codes[:].bitcast(FP8X4), scales=h_scales[:], in_=h_grouped_tiles[pair][:]
+                out=h_codes[:].bitcast(FP8X4), scales=h_scales[:], in_=h_grouped_tiles[group][:]
             )
-            h_quantised[pair] = (h_codes, h_scales)
+            for i in range(len(group)):
+                h_quantised[group[i]] = (h_codes[:, i * P : (i + 1) * P], h_scales[:, i * P : (i + 1) * P])
 
         results = {}
 
         def product(pair, w, c, j, engine):
-            h_codes, h_scales = h_quantised[pair]
+            h_codes, h_scales = h_quantised[2 * pair + j]
             w_codes, w_scales = w_quantised[w * CHUNKS + c]
             bias_cols = bias_all[:, (w * CHUNKS + c) * BANK : (w * CHUNKS + c + 1) * BANK]
-            rows = slice(j * P, (j + 1) * P)
             if (pair, w) not in results:
                 results[pair, w] = out_pool.tile([P, 2, FEATURES], F32, name="result")
             acc = acc_psum.tile([P, BANK], F32, tag="acc")
             nc.tensor.matmul_mx(
                 out=acc[:],
-                lhsT=h_codes[:, rows].bitcast(FP8X4),
-                lhsT_scale=h_scales[:, rows],
+                lhsT=h_codes.bitcast(FP8X4),
+                lhsT_scale=h_scales,
                 rhs=w_codes[:].bitcast(FP8X4),
                 rhs_scale=w_scales[:],
                 start=True,
@@ -222,15 +229,16 @@ def tile_wiaa_pa_kernel(tc, x, Wq, bq, Wk, bk, out_q, out_k):
         def store(pair, w):
             nc.sync.dma_start(out=out_rows[w][:, 2 * pair : 2 * pair + 2, :], in_=results[pair, w][:])
 
-        turn_bias()
         flip_h(0)
+        turn_bias()
         flip_weight(0, 0, nc.vector)
-        flip_h(1)
         flip_weight(0, 1, nc.scalar)
+        flip_h(1)
         quantise_h(0)
         quantise_weight(0)
+        quantise_h(1)
         flip_weight(1, 0, nc.scalar)
-        flip_weight(1, 1, nc.scalar)
+        flip_weight(1, 1, nc.vector)
         spread_bias(0)
         product(0, 0, 0, 0, nc.scalar)
         quantise_weight(1)
@@ -241,7 +249,7 @@ def tile_wiaa_pa_kernel(tc, x, Wq, bq, Wk, bk, out_q, out_k):
         product(0, 0, 1, 1, nc.vector)
         store(0, 0)
         flip_weight(2, 0, nc.scalar)
-        quantise_h(1)
+        quantise_h(2)
         flip_weight(2, 1, nc.scalar)
         product(1, 0, 0, 0, nc.vector)
         flip_weight(3, 0, nc.scalar)
@@ -260,7 +268,7 @@ def tile_wiaa_pa_kernel(tc, x, Wq, bq, Wk, bk, out_q, out_k):
         product(0, 1, 1, 0, nc.vector)
         product(0, 1, 1, 1, nc.vector)
         store(0, 1)
-        quantise_h(2)
+        quantise_h(4)
         product(1, 1, 0, 0, nc.scalar)
         product(1, 1, 0, 1, nc.vector)
         product(1, 1, 1, 0, nc.vector)
@@ -273,11 +281,10 @@ def tile_wiaa_pa_kernel(tc, x, Wq, bq, Wk, bk, out_q, out_k):
                     flip_h(2 * pair + 2)
                     flip_h(2 * pair + 3)
                 if w == 1 and pair + 1 < PAIRS:
-                    quantise_h(pair + 1)
+                    quantise_h(2 * pair + 2)
                 if w == 0 and 2 * pair + 4 in SUMMED_BY_GPSIMD:
                     sum_sample_pairs(2 * pair + 4)
                 for c in range(CHUNKS):
                     for j in range(2):
-                        on_scalar = j == 0 and (c == 0 or (w == 1 and pair % 2 == 1 and pair + 1 < PAIRS))
-                        product(pair, w, c, j, nc.scalar if on_scalar else nc.vector)
+                        product(pair, w, c, j, nc.scalar if c == 0 and j == 0 else nc.vector)
                 store(pair, w)

@@ -226,8 +226,8 @@ def tile_wiaa_pa_kernel(tc, x, Wq, bq, Wk, bk, out_q, out_k):
             else:
                 nc.vector.tensor_tensor(out=finished, in0=acc[:], in1=bias_cols, op=ADD)
 
-        def store(pair, w):
-            nc.sync.dma_start(out=out_rows[w][:, 2 * pair : 2 * pair + 2, :], in_=results[pair, w][:])
+        def store(pair, w, queue=nc.sync):
+            queue.dma_start(out=out_rows[w][:, 2 * pair : 2 * pair + 2, :], in_=results[pair, w][:])
 
         flip_h(0)
         turn_bias()
@@ -273,7 +273,6 @@ def tile_wiaa_pa_kernel(tc, x, Wq, bq, Wk, bk, out_q, out_k):
         product(1, 1, 0, 1, nc.vector)
         product(1, 1, 1, 0, nc.vector)
         product(1, 1, 1, 1, nc.vector)
-        store(1, 1)
 
         for pair in range(2, PAIRS):
             for w in range(2):
@@ -287,4 +286,7 @@ def tile_wiaa_pa_kernel(tc, x, Wq, bq, Wk, bk, out_q, out_k):
                 for c in range(CHUNKS):
                     for j in range(2):
                         product(pair, w, c, j, nc.scalar if c == 0 and j == 0 else nc.vector)
-                store(pair, w)
+                        if w == 0 and c == 0 and j == 0:
+                            store(pair - 1, 1, nc.scalar)
+                if w == 0 or pair + 1 == PAIRS:
+                    store(pair, w)

@@ -60,25 +60,25 @@ def tile_wiaa_pa_kernel(tc, x, Wq, bq, Wk, bk, out_q, out_k):
             nc.sync.dma_start(out=x_group[:], in_=x_rows[:, first : first + count, :])
             x_tiles.extend(x_group[:, i, :] for i in range(count))
 
-        def load_weight(w, c):
-            w_chunks = weights[w].rearrange("(c p a) i -> c p a i", a=BANK // P, p=P)
-            w_raw = w_pool.tile([P, BANK // P, COEFFS], BF16, name="w_raw")
-            nc.sync.dma_start(out=w_raw[:], in_=w_chunks[c])
-            w_raws.append(w_raw)
+        def load_weight(w, first, count):
+            w_chunks = weights[w].rearrange("(c p a) i -> p c (a i)", a=BANK // P, p=P)
+            w_raw = w_pool.tile([P, count, BANK // P * COEFFS], BF16, name="w_raw%d" % count)
+            nc.sync.dma_start(out=w_raw[:], in_=w_chunks[:, first : first + count, :])
+            for c in range(count):
+                w_raws.append(w_raw[:, c, :].rearrange("p (a i) -> p a i", i=COEFFS))
 
         load_x(0, 1)
         bias_in = const.tile([2 * FEATURES // P, P], BF16)
         for w in range(2):
-            nc.sync.dma_start(
+            nc.scalar.dma_start(
                 out=bias_in[w * FEATURES // P : (w + 1) * FEATURES // P, :],
                 in_=biases[w].rearrange("(r f) -> r f", f=P),
             )
-        load_weight(0, 0)
+        load_weight(0, 0, 1)
         load_x(1, 1)
-        load_weight(0, 1)
+        load_weight(0, 1, 1)
         load_x(2, 2)
-        load_weight(1, 0)
-        load_weight(1, 1)
+        load_weight(1, 0, 2)
         load_x(4, 4)
         load_x(8, 8)
 
@@ -98,7 +98,6 @@ def tile_wiaa_pa_kernel(tc, x, Wq, bq, Wk, bk, out_q, out_k):
                 nc.vector.tensor_copy(out=out, in_=in_)
 
         def turn_bias():
-            nc.vector.tensor_copy(out=bias_rows[0 : 2 * FEATURES // P, :], in_=bias_in[:])
             turned = acc_psum.tile([P, P], BF16, tag="acc")
             nc.tensor.transpose(out=turned[:], in_=bias_rows[:], identity=identity_bf[:])
             nc.vector.tensor_copy(out=bias_columns[:], in_=turned[:])
@@ -230,9 +229,10 @@ def tile_wiaa_pa_kernel(tc, x, Wq, bq, Wk, bk, out_q, out_k):
             queue.dma_start(out=out_rows[w][:, 2 * pair : 2 * pair + 2, :], in_=results[pair, w][:])
 
         flip_h(0)
-        turn_bias()
+        nc.vector.tensor_copy(out=bias_rows[0 : 2 * FEATURES // P, :], in_=bias_in[:])
         flip_weight(0, 0, nc.vector)
         flip_weight(0, 1, nc.scalar)
+        turn_bias()
         flip_h(1)
         quantise_h(0)
         quantise_weight(0)

import math
from contextlib import ExitStack

import concourse.mybir as mybir
from concourse.masks import make_identity

F32 = mybir.dt.float32
BF16 = mybir.dt.bfloat16
U32 = mybir.dt.uint32
U8 = mybir.dt.uint8
FP8X4 = mybir.dt.float8_e4m3fn_x4
ADD = mybir.AluOpType.add
COPY = mybir.ActivationFunctionType.Copy

P = 128
PACK = 4
ROWS = 2048
SAMPLES = 1024
COEFFS = SAMPLES // 2
FEATURES = 1024
BANK = 512
ROW_TILES = ROWS // P
PAIRS = ROW_TILES // 2
CHUNKS = FEATURES // BANK
INV_SQRT2 = 1.0 / math.sqrt(2.0)

SUMMED_BY_GPSIMD = (8, 10, 12, 14)

FLOPS = 2 * ROWS * COEFFS * 2 * FEATURES


def tile_wiaa_pa_kernel(tc, x, Wq, bq, Wk, bk, out_q, out_k):
    nc = tc.nc
    weights = (Wq, Wk)
    biases = (bq, bk)

    x_rows = x.flatten_outer_dims().rearrange("(p j) n -> p j n", j=ROW_TILES)
    out_rows = tuple(
        o.flatten_outer_dims().rearrange("(p j) f -> p j f", j=ROW_TILES) for o in (out_q, out_k)
    )

    with ExitStack() as ctx:
        const = ctx.enter_context(tc.tile_pool(name="const", bufs=1))
        x_pool = ctx.enter_context(tc.tile_pool(name="x_pool", bufs=1))
        w_pool = ctx.enter_context(tc.tile_pool(name="w_pool", bufs=2 * CHUNKS))
        w_stage = ctx.enter_context(tc.tile_pool(name="w_stage", bufs=2))
        sum_pool = ctx.enter_context(tc.tile_pool(name="sum_pool", bufs=4))
        h_stage = ctx.enter_context(tc.tile_pool(name="h_stage", bufs=4))
        out_pool = ctx.enter_context(tc.tile_pool(name="out_pool", bufs=10))
        flip_psum = ctx.enter_context(tc.psum_pool(name="flip_psum", bufs=4))
        acc_psum = ctx.enter_context(tc.psum_pool(name="acc_psum", bufs=4))

        ctx.enter_context(tc.manual_schedule())

        x_tiles = []
        w_raws = []

        def load_x(first, count):
            x_group = x_pool.tile([P, count, SAMPLES], BF16, name="x_group%d" % first)
            nc.sync.dma_start(out=x_group[:], in_=x_rows[:, first : first + count, :])
            x_tiles.extend(x_group[:, i, :] for i in range(count))

        def load_weight(w, first, count):
            w_chunks = weights[w].rearrange("(c p a) i -> p c (a i)", a=BANK // P, p=P)
            w_raw = w_pool.tile([P, count, BANK // P * COEFFS], BF16, name="w_raw%d" % count)
            nc.sync.dma_start(out=w_raw[:], in_=w_chunks[:, first : first + count, :])
            for c in range(count):
                w_raws.append(w_raw[:, c, :].rearrange("p (a i) -> p a i", i=COEFFS))

        load_x(0, 1)
        bias_in = const.tile([2 * FEATURES // P, P], BF16)
        for w in range(2):
            nc.scalar.dma_start(
                out=bias_in[w * FEATURES // P : (w + 1) * FEATURES // P, :],
                in_=biases[w].rearrange("(r f) -> r f", f=P),
            )
        load_weight(0, 0, 1)
        load_x(1, 1)
        load_weight(0, 1, 1)
        load_x(2, 2)
        load_weight(1, 0, 2)
        load_x(4, 4)
        load_x(8, 8)

        identity_bf = const.tile([P, P], BF16)
        make_identity(nc, identity_bf[:])
        identity = const.tile([P, P], F32)
        bias_rows = const.tile([P, P], BF16)
        nc.vector.memset(bias_rows[:], 0.0)
        nc.vector.tensor_copy(out=identity[:], in_=identity_bf[:])
        bias_columns = const.tile([P, P], BF16)
        bias_all = const.tile([P, 2 * FEATURES], BF16)

        def copy_out(engine, out, in_):
            if engine is nc.scalar:
                nc.scalar.copy(out=out, in_=in_)
            else:
                nc.vector.tensor_copy(out=out, in_=in_)

        def turn_bias():
            turned = acc_psum.tile([P, P], BF16, tag="acc")
            nc.tensor.transpose(out=turned[:], in_=bias_rows[:], identity=identity_bf[:])
            nc.vector.tensor_copy(out=bias_columns[:], in_=turned[:])

        def spread_bias(w):
            spread = acc_psum.tile([P, FEATURES], BF16, tag="acc")
            for r in range(FEATURES // P):
                column = w * FEATURES // P + r
                nc.tensor.transpose(
                    out=spread[:, r * P : (r + 1) * P],
                    in_=bias_columns[:, column : column + 1].to_broadcast([P, P]),
                    identity=identity_bf[:],
                )
            nc.scalar.copy(out=bias_all[:, w * FEATURES : (w + 1) * FEATURES], in_=spread[:])

        w_grouped_tiles = {}
        w_quantised = {}

        def flip_weight(chunk, half, engine):
            if half == 0:
                w_grouped_tiles[chunk] = w_stage.tile([P, BANK * PACK], BF16, align_bytes=64, name="w_grouped")
            grouped_words = w_grouped_tiles[chunk][:].bitcast(F32).rearrange("p (m h v) -> p m h v", h=2, v=4)
            flipped = flip_psum.tile([P, 4, P], F32, tag="flip")
            for a in range(2):
                words = w_raws[chunk][:, 2 * half + a, :].bitcast(F32)
                for u in range(2):
                    nc.tensor.transpose(
                        out=flipped[:, 2 * a + u, :],
                        in_=words[:, u * P : (u + 1) * P],
                        identity=identity[:],
                    )
            copy_out(engine, grouped_words[:, :, half, :], flipped[:].rearrange("p v m -> p m v"))

        def quantise_weight(chunk):
            w_codes = w_pool.tile([P, BANK], U32, align_bytes=64, name="w_codes")
            w_scales = w_pool.tile([P, BANK], U8, align_bytes=64, name="w_scales")
            nc.vector.quantize_mx(
                out=w_codes[:].bitcast(FP8X4), scales=w_scales[:], in_=w_grouped_tiles[chunk][:]
            )
            w_quantised[chunk] = (w_codes, w_scales)

        sums = {}

        def sum_sample_pairs(tile):
            samples = x_tiles[tile].rearrange("r (u p e s) -> r u e p s", u=2, p=P, e=2, s=2)
            sums[tile] = sum_pool.tile([P, COEFFS], F32, name="sums")
            nc.gpsimd.tensor_tensor(
                out=sums[tile][:].rearrange("r (u e p) -> r u e p", u=2, e=2),
                in0=samples[:, :, :, :, 0],
                in1=samples[:, :, :, :, 1],
                op=ADD,
            )

        def h_group(tile):
            return (tile,) if tile < 2 else (tile - tile % 2, tile - tile % 2 + 1)

        h_grouped_tiles = {}
        h_quantised = {}

        def flip_h(tile):
            group = h_group(tile)
            if tile == group[0]:
                name = "h_grouped%d" % len(group)
                h_grouped_tiles[group] = h_stage.tile([P, len(group) * P * PACK], BF16, align_bytes=64, name=name)
            h_grouped = h_grouped_tiles[group]
            i = tile - group[0]
            flipped = flip_psum.tile([P, PACK, P], F32, tag="flip")
            if tile in sums:
                for t in range(PACK):
                    nc.tensor.transpose(
                        out=flipped[:, t, :],
                        in_=sums[tile][:, t * P : (t + 1) * P],
                        identity=identity[:],
                    )
            else:
                samples = x_tiles[tile].rearrange("r (u p e s) -> r u e s p", u=2, p=P, e=2, s=2)
                for t in range(PACK):
                    for s in range(2):
                        nc.tensor.matmul(
                            out=flipped[:, t, :],
                            lhsT=samples[:, t // 2, t % 2, s, :],
                            rhs=identity_bf[:],
                            start=(s == 0),
                            stop=(s == 1),
                        )
            nc.scalar.activation(
                out=h_grouped[:, i * P * PACK : (i + 1) * P * PACK].rearrange("p (r t) -> p r t", t=PACK),
                in_=flipped[:].rearrange("p t r -> p r t"),
                func=COPY,
                scale=INV_SQRT2,
            )

        def quantise_h(tile):
            group = h_group(tile)
            h_codes = h_stage.tile([P, len(group) * P], U32, align_bytes=64, name="h_codes%d" % len(group))
            h_scales = h_stage.tile([P, len(group) * P], U8, align_bytes=64, name="h_scales%d" % len(group))
            nc.vector.quantize_mx(
                out=h_codes[:].bitcast(FP8X4), scales=h_scales[:], in_=h_grouped_tiles[group][:]
            )
            for i in range(len(group)):
                h_quantised[group[i]] = (h_codes[:, i * P : (i + 1) * P], h_scales[:, i * P : (i + 1) * P])

        results = {}

        def product(pair, w, c, j, engine):
            h_codes, h_scales = h_quantised[2 * pair + j]
            w_codes, w_scales = w_quantised[w * CHUNKS + c]
            bias_cols = bias_all[:, (w * CHUNKS + c) * BANK : (w * CHUNKS + c + 1) * BANK]
            if (pair, w) not in results:
                results[pair, w] = out_pool.tile([P, 2, FEATURES], F32, name="result")
            acc = acc_psum.tile([P, BANK], F32, tag="acc")
            nc.tensor.matmul_mx(
                out=acc[:],
                lhsT=h_codes.bitcast(FP8X4),
                lhsT_scale=h_scales,
                rhs=w_codes[:].bitcast(FP8X4),
                rhs_scale=w_scales[:],
                start=True,
                stop=True,
            )
            finished = results[pair, w][:, j, c * BANK : (c + 1) * BANK]
            if engine is nc.scalar:
                nc.scalar.copy(out=finished, in_=acc[:])
                nc.gpsimd.tensor_tensor(out=finished, in0=finished, in1=bias_cols, op=ADD)
            else:
                nc.vector.tensor_tensor(out=finished, in0=acc[:], in1=bias_cols, op=ADD)

        def store(pair, w, queue=nc.sync):
            queue.dma_start(out=out_rows[w][:, 2 * pair : 2 * pair + 2, :], in_=results[pair, w][:])

        flip_h(0)
        nc.vector.tensor_copy(out=bias_rows[0 : 2 * FEATURES // P, :], in_=bias_in[:])
        flip_weight(0, 0, nc.vector)
        flip_weight(0, 1, nc.scalar)
        turn_bias()
        flip_h(1)
        quantise_h(0)
        quantise_weight(0)
        quantise_h(1)
        flip_weight(1, 0, nc.scalar)
        flip_weight(1, 1, nc.vector)
        spread_bias(0)
        product(0, 0, 0, 0, nc.scalar)
        quantise_weight(1)
        product(0, 0, 0, 1, nc.vector)
        flip_h(2)
        flip_h(3)
        product(0, 0, 1, 0, nc.vector)
        product(0, 0, 1, 1, nc.vector)
        store(0, 0)
        flip_weight(2, 0, nc.scalar)
        quantise_h(2)
        flip_weight(2, 1, nc.scalar)
        product(1, 0, 0, 0, nc.vector)
        flip_weight(3, 0, nc.scalar)
        flip_weight(3, 1, nc.scalar)
        quantise_weight(2)
        product(1, 0, 0, 1, nc.vector)
        product(1, 0, 1, 0, nc.vector)
        quantise_weight(3)
        product(1, 0, 1, 1, nc.vector)
        store(1, 0)
        spread_bias(1)
        product(0, 1, 0, 0, nc.scalar)
        product(0, 1, 0, 1, nc.vector)
        flip_h(4)
        flip_h(5)
        product(0, 1, 1, 0, nc.vector)
        product(0, 1, 1, 1, nc.vector)
        store(0, 1)
        quantise_h(4)
        product(1, 1, 0, 0, nc.scalar)
        product(1, 1, 0, 1, nc.vector)
        product(1, 1, 1, 0, nc.vector)
        product(1, 1, 1, 1, nc.vector)

        for pair in range(2, PAIRS):
            for w in range(2):
                if w == 0 and pair + 1 < PAIRS:
                    flip_h(2 * pair + 2)
                    flip_h(2 * pair + 3)
                if w == 1 and pair + 1 < PAIRS:
                    quantise_h(2 * pair + 2)
                if w == 0 and 2 * pair + 4 in SUMMED_BY_GPSIMD:
                    sum_sample_pairs(2 * pair + 4)
                for c in range(CHUNKS):
                    for j in range(2):
                        product(pair, w, c, j, nc.scalar if c == 0 and j == 0 else nc.vector)
                        if w == 0 and c == 0 and j == 0:
                            store(pair - 1, 1, nc.scalar)
                if w == 0 or pair + 1 == PAIRS:
                    store(pair, w)
